import numpy as np
import ml_dtypes


def mxq(x, axis, fmt="e4m3"):
    dtype, down = {"e4m3": (ml_dtypes.float8_e4m3fn, 7), "e5m2": (ml_dtypes.float8_e5m2, 14)}[fmt]
    v = np.moveaxis(np.asarray(x, np.float32).astype(ml_dtypes.bfloat16).astype(np.float64), axis, -1)
    blocks = v.reshape(v.shape[:-1] + (-1, 32))
    amax = np.abs(blocks).max(-1, keepdims=True)
    byte = np.maximum(np.where(amax > 0, np.frexp(amax)[1] - 1 + 127, 0) - down, 1)
    scale = np.exp2(byte - 127.0)
    codes = (blocks / scale).astype(np.float32).astype(dtype).astype(np.float64)
    return np.moveaxis((codes * scale).reshape(v.shape), -1, axis)


WIDE = False


def mx_kscale(k):
    if not WIDE:
        return np.ones(k)
    levels = np.array([10, -10, 5, -5, 0])
    a = np.random.permutation(np.resize(levels, k // 512 * 4)).reshape(k // 512, 4)
    idx = np.arange(k)
    return np.exp2(a[idx // 512, idx % 128 // 32])


BF16 = ml_dtypes.bfloat16


def bf(x):
    return np.asarray(x, np.float32).astype(BF16)


def f64(x):
    return np.asarray(x).astype(np.float64)


B, N, DIM, H, DH = 2, 256, 1536, 16, 96
D1 = DH // 3


def rotate_half(t):
    d = t.shape[-1]
    t1, t2 = t[..., : (d + 1) // 2], t[..., (d + 1) // 2:]
    return np.concatenate((-t2, t1), axis=-1)


def apply_rope(t, freqs):
    return t * np.cos(freqs) + rotate_half(t) * np.sin(freqs)


def rope3(t, fs):
    return np.concatenate([apply_rope(ts, f) for ts, f in zip(np.split(t, (D1, 2 * D1), axis=-1), fs)], axis=-1)


def setup_inputs():
    s = mx_kscale(DIM)
    return {"x": bf(np.random.standard_normal((B, N, DIM)) * s),
            "f1": bf(np.random.uniform(0.0, 1.0, (N, D1))),
            "f2": bf(np.random.uniform(0.0, 1.0, (N, D1))),
            "f3": bf(np.random.uniform(0.0, 1.0, (N, D1))),
            "Wqkv": bf(np.random.standard_normal((DIM, 3 * H * DH)) / np.sqrt(DIM) / s[:, None])}


def reference(x, f1, f2, f3, Wqkv):
    qkv = mxq(f64(x), 2, "e4m3") @ mxq(f64(Wqkv), 0, "e4m3")
    q, k, v = np.split(qkv, 3, axis=-1)
    to_heads = lambda t: t.reshape(B, N, H, DH).transpose(0, 2, 1, 3)
    q, k, v = to_heads(q), to_heads(k), to_heads(v)
    fs = (f64(f1), f64(f2), f64(f3))
    return rope3(q, fs), rope3(k, fs), v

@@ -1,0 +1,222 @@
+import math
+from contextlib import ExitStack
+
+import concourse.mybir as mybir
+from concourse.masks import make_identity
+
+F32 = mybir.dt.float32
+BF16 = mybir.dt.bfloat16
+U32 = mybir.dt.uint32
+U8 = mybir.dt.uint8
+FP8X4 = mybir.dt.float8_e4m3fn_x4
+MULT = mybir.AluOpType.mult
+ADD = mybir.AluOpType.add
+SIN = mybir.ActivationFunctionType.Sin
+
+BATCH, TOKENS, DIM, HEADS, HEAD_DIM = 2, 256, 1536, 16, 96
+SECTIONS = 3
+ROPE_SECTIONS = 2
+AXES, AXIS_DIM, HALF = 3, 32, 16
+
+P = 128
+PACK = 4
+K_PASS = P * PACK
+PASSES = DIM // K_PASS
+PAIR = TOKENS // P
+
+UNIT_HEADS = 4
+UNIT = UNIT_HEADS * HEAD_DIM
+WIDE, NARROW = 256, 128
+UNITS_PER_SECTION = HEADS // UNIT_HEADS
+UNITS = SECTIONS * UNITS_PER_SECTION
+LOAD_UNITS = 2
+LOAD_COLS = LOAD_UNITS * UNIT
+LOADS = UNITS // LOAD_UNITS
+AHEAD = 2
+BANK = 512
+
+FLOPS = 2 * BATCH * TOKENS * DIM * SECTIONS * HEADS * HEAD_DIM
+
+
+def tile_attention_pa_kernel(tc, x, f1, f2, f3, Wqkv, out_0, out_1, out_2):
+    nc = tc.nc
+    outs = (out_0, out_1, out_2)
+
+    with ExitStack() as ctx:
+        const = ctx.enter_context(tc.tile_pool(name="const", bufs=1))
+        stage = ctx.enter_context(tc.tile_pool(name="stage", bufs=3))
+        packed = ctx.enter_context(tc.tile_pool(name="packed", bufs=4))
+        result = ctx.enter_context(tc.tile_pool(name="result", bufs=6))
+        scratch = ctx.enter_context(tc.tile_pool(name="scratch", bufs=3))
+        psum = ctx.enter_context(tc.psum_pool(name="psum", bufs=8))
+
+        x_sb = const.tile([P, BATCH, PAIR * DIM], BF16)
+        w_raw = [
+            const.tile([P, PASSES, PACK, LOAD_COLS], BF16, name="w_raw%d" % load)
+            for load in range(LOADS)
+        ]
+
+        def load_x(b):
+            nc.sync.dma_start(out=x_sb[:, b, :], in_=x[b].rearrange("(p e) k -> p (e k)", e=PAIR))
+
+        def load_weights(load):
+            cols = slice(load * LOAD_COLS, (load + 1) * LOAD_COLS)
+            for g in range(PASSES):
+                rows = slice(g * K_PASS, (g + 1) * K_PASS)
+                nc.sync.dma_start(
+                    out=w_raw[load][:, g, :, :],
+                    in_=Wqkv[rows, cols].rearrange("(p j) w -> p j w", j=PACK),
+                )
+
+        angles = const.tile([P, PAIR, AXES, AXIS_DIM], BF16)
+        for axis, f in enumerate((f1, f2, f3)):
+            nc.scalar.dma_start(
+                out=angles[:, :, axis, :], in_=f.rearrange("(p e) c -> p e c", e=PAIR)
+            )
+
+        load_x(0)
+        load_weights(0)
+        load_x(1)
+        for load in range(1, LOADS):
+            load_weights(load)
+
+        cos_t = const.tile([P, PAIR, AXES, 2, HALF], F32)
+        sin_t = const.tile([P, PAIR, AXES, 2, HALF], F32)
+        angle_halves = angles[:].rearrange("p e a (s i) -> p (e a) s i", s=2)
+        sin_halves = sin_t[:].rearrange("p e a s i -> p (e a) s i")
+        nc.scalar.activation(
+            out=cos_t[:].rearrange("p e a s i -> p (e a s i)"),
+            in_=angles[:].rearrange("p e a c -> p (e a c)"),
+            func=SIN,
+            scale=-1.0,
+            bias=math.pi / 2,
+        )
+        nc.scalar.activation(
+            out=sin_halves[:, :, 0, :], in_=angle_halves[:, :, 0, :], func=SIN, scale=-1.0
+        )
+        nc.scalar.activation(out=sin_halves[:, :, 1, :], in_=angle_halves[:, :, 1, :], func=SIN)
+
+        ident = const.tile([P, P], F32)
+        make_identity(nc, ident[:])
+        x_words = x_sb[:].bitcast(F32).rearrange(
+            "p b (e g q u) -> p b e g u q", e=PAIR, g=PASSES, u=2
+        )
+        x_grouped = const.tile([P, PASSES * BATCH * PAIR * P * PACK], BF16, align_bytes=64)
+        x_grouped_words = x_grouped[:].bitcast(F32).rearrange(
+            "p (g b e t u) -> p g b e t u", g=PASSES, b=BATCH, e=PAIR, u=2
+        )
+        x_grouped_cols = x_grouped[:].rearrange("p (g b c) -> p g b c", g=PASSES, b=BATCH)
+        x_codes = const.tile([P, PASSES, BATCH, PAIR * P], U32, align_bytes=64)
+        x_scales = const.tile([P, PASSES, BATCH, PAIR * P], U8, align_bytes=64)
+        for b in range(BATCH):
+            for g in range(PASSES):
+                turned = psum.tile([P, BANK], F32, name="bank")
+                turned_words = turned[:].rearrange("p (e u t) -> p e u t", e=PAIR, u=2)
+                for e in range(PAIR):
+                    for u in range(2):
+                        nc.tensor.transpose(
+                            turned_words[:, e, u, :], x_words[:, b, e, g, u, :], ident[:]
+                        )
+                nc.vector.tensor_copy(
+                    out=x_grouped_words[:, g, b],
+                    in_=turned_words.rearrange("p e u t -> p e t u"),
+                )
+            for g in range(PASSES):
+                nc.vector.quantize_mx(
+                    out=x_codes[:, g, b, :].bitcast(FP8X4),
+                    scales=x_scales[:, g, b, :],
+                    in_=x_grouped_cols[:, g, b, :],
+                )
+
+        def prepare(unit):
+            raw = w_raw[unit // LOAD_UNITS]
+            cols = slice((unit % LOAD_UNITS) * UNIT, (unit % LOAD_UNITS + 1) * UNIT)
+            grouped = stage.tile([P, PASSES, UNIT, PACK], BF16, align_bytes=64)
+            codes = packed.tile([P, PASSES, UNIT], U32, align_bytes=64)
+            scales = packed.tile([P, PASSES, UNIT], U8, align_bytes=64)
+            for g in range(PASSES):
+                src = raw[:, g, :, cols].rearrange("p j (c i) -> p c j i", i=4)
+                dst = grouped[:, g, :, :].rearrange("p (c i) j -> p c j i", i=4)
+                if unit < LOAD_UNITS and g > 0:
+                    nc.vector.tensor_copy(out=dst, in_=src)
+                else:
+                    nc.scalar.copy(out=dst, in_=src)
+            for g in range(PASSES):
+                for part in (slice(0, WIDE), slice(WIDE, UNIT)):
+                    nc.vector.quantize_mx(
+                        out=codes[:, g, part].bitcast(FP8X4),
+                        scales=scales[:, g, part],
+                        in_=grouped[:, g, part, :].rearrange("p w j -> p (w j)"),
+                    )
+            return codes, scales
+
+        def multiply(codes, scales, b, e):
+            bank = psum.tile([P, BANK], F32, name="bank")
+            tokens = slice(e * P, (e + 1) * P)
+            for part in (slice(0, WIDE), slice(WIDE, UNIT)):
+                for g in range(PASSES):
+                    nc.tensor.matmul_mx(
+                        out=bank[:, part],
+                        lhsT=x_codes[:, g, b, tokens].bitcast(FP8X4),
+                        lhsT_scale=x_scales[:, g, b, tokens],
+                        rhs=codes[:, g, part].bitcast(FP8X4),
+                        rhs_scale=scales[:, g, part],
+                        start=(g == 0),
+                        stop=(g == PASSES - 1),
+                    )
+            return bank
+
+        def rotate(banks, rotated):
+            crossed = scratch.tile([P, UNIT_HEADS, PAIR, HEAD_DIM], F32)
+            for e in range(PAIR):
+                t = banks[e][:, 0:UNIT]
+                nc.vector.tensor_tensor(
+                    out=rotated[:, :, e, :],
+                    in0=t.rearrange("p (h d) -> p h d", h=UNIT_HEADS),
+                    in1=cos_t[:, e].rearrange("p a s i -> p (a s i)").unsqueeze(1).to_broadcast(
+                        [P, UNIT_HEADS, HEAD_DIM]
+                    ),
+                    op=MULT,
+                )
+                t_halves = t.rearrange("p (h a s i) -> p h a s i", h=UNIT_HEADS, a=AXES, s=2)
+                crossed_halves = crossed[:, :, e, :].rearrange(
+                    "p h (a s i) -> p h a s i", a=AXES, s=2
+                )
+                for s in range(2):
+                    nc.vector.tensor_tensor(
+                        out=crossed_halves[:, :, :, s, :],
+                        in0=t_halves[:, :, :, 1 - s, :],
+                        in1=sin_t[:, e, :, s, :].unsqueeze(1).to_broadcast(
+                            [P, UNIT_HEADS, AXES, HALF]
+                        ),
+                        op=MULT,
+                    )
+            nc.vector.tensor_tensor(out=rotated[:], in0=rotated[:], in1=crossed[:], op=ADD)
+
+        def finish(unit, codes, scales):
+            section = unit // UNITS_PER_SECTION
+            head = (unit % UNITS_PER_SECTION) * UNIT_HEADS
+            for b in range(BATCH):
+                banks = [multiply(codes, scales, b, e) for e in range(PAIR)]
+                done = result.tile([P, UNIT_HEADS, PAIR, HEAD_DIM], F32)
+                if section < ROPE_SECTIONS:
+                    rotate(banks, done)
+                else:
+                    for e in range(PAIR):
+                        nc.scalar.copy(
+                            out=done[:, :, e, :],
+                            in_=banks[e][:, 0:UNIT].rearrange("p (h d) -> p h d", h=UNIT_HEADS),
+                        )
+                nc.sync.dma_start(
+                    out=outs[section][b, head : head + UNIT_HEADS].rearrange(
+                        "h (p e) d -> p h (e d)", e=PAIR
+                    ),
+                    in_=done[:].rearrange("p h e d -> p h (e d)"),
+                )
+
+        ready = [prepare(unit) for unit in range(AHEAD)]
+        for unit in range(UNITS):
+            if unit + AHEAD < UNITS:
+                ready.append(prepare(unit + AHEAD))
+            codes, scales = ready[unit]
+            finish(unit, codes, scales)

@@ -16,7 +16,7 @@ SIN = mybir.ActivationFunctionType.Sin
 BATCH, TOKENS, DIM, HEADS, HEAD_DIM = 2, 256, 1536, 16, 96
 SECTIONS = 3
 ROPE_SECTIONS = 2
-AXES, AXIS_DIM, HALF = 3, 32, 16
+AXES, HALF = 3, 16
 
 P = 128
 PACK = 4
@@ -26,13 +26,13 @@ PAIR = TOKENS // P
 
 UNIT_HEADS = 4
 UNIT = UNIT_HEADS * HEAD_DIM
-WIDE, NARROW = 256, 128
+WIDE = 256
 UNITS_PER_SECTION = HEADS // UNIT_HEADS
-UNITS = SECTIONS * UNITS_PER_SECTION
 LOAD_UNITS = 2
 LOAD_COLS = LOAD_UNITS * UNIT
-LOADS = UNITS // LOAD_UNITS
-AHEAD = 2
+LOADS = SECTIONS * UNITS_PER_SECTION // LOAD_UNITS
+ROPE_LOADS = ROPE_SECTIONS * UNITS_PER_SECTION // LOAD_UNITS
+QUANT_COLS = 512
 BANK = 512
 
 FLOPS = 2 * BATCH * TOKENS * DIM * SECTIONS * HEADS * HEAD_DIM
@@ -44,11 +44,12 @@ def tile_attention_pa_kernel(tc, x, f1, f2, f3, Wqkv, out_0, out_1, out_2):
 
     with ExitStack() as ctx:
         const = ctx.enter_context(tc.tile_pool(name="const", bufs=1))
-        stage = ctx.enter_context(tc.tile_pool(name="stage", bufs=3))
-        packed = ctx.enter_context(tc.tile_pool(name="packed", bufs=4))
+        stage = ctx.enter_context(tc.tile_pool(name="stage", bufs=4))
+        packed = ctx.enter_context(tc.tile_pool(name="packed", bufs=3))
         result = ctx.enter_context(tc.tile_pool(name="result", bufs=6))
         scratch = ctx.enter_context(tc.tile_pool(name="scratch", bufs=3))
         psum = ctx.enter_context(tc.psum_pool(name="psum", bufs=8))
+        ctx.enter_context(tc.manual_schedule())
 
         x_sb = const.tile([P, BATCH, PAIR * DIM], BF16)
         w_raw = [
@@ -68,7 +69,7 @@ def tile_attention_pa_kernel(tc, x, f1, f2, f3, Wqkv, out_0, out_1, out_2):
                     in_=Wqkv[rows, cols].rearrange("(p j) w -> p j w", j=PACK),
                 )
 
-        angles = const.tile([P, PAIR, AXES, AXIS_DIM], BF16)
+        angles = const.tile([P, PAIR, AXES, 2 * HALF], BF16)
         for axis, f in enumerate((f1, f2, f3)):
             nc.scalar.dma_start(
                 out=angles[:, :, axis, :], in_=f.rearrange("(p e) c -> p e c", e=PAIR)
@@ -108,7 +109,8 @@ def tile_attention_pa_kernel(tc, x, f1, f2, f3, Wqkv, out_0, out_1, out_2):
         x_grouped_cols = x_grouped[:].rearrange("p (g b c) -> p g b c", g=PASSES, b=BATCH)
         x_codes = const.tile([P, PASSES, BATCH, PAIR * P], U32, align_bytes=64)
         x_scales = const.tile([P, PASSES, BATCH, PAIR * P], U8, align_bytes=64)
-        for b in range(BATCH):
+
+        def turn_x(b):
             for g in range(PASSES):
                 turned = psum.tile([P, BANK], F32, name="bank")
                 turned_words = turned[:].rearrange("p (e u t) -> p e u t", e=PAIR, u=2)
@@ -128,39 +130,44 @@ def tile_attention_pa_kernel(tc, x, f1, f2, f3, Wqkv, out_0, out_1, out_2):
                     in_=x_grouped_cols[:, g, b, :],
                 )
 
-        def prepare(unit):
-            raw = w_raw[unit // LOAD_UNITS]
-            cols = slice((unit % LOAD_UNITS) * UNIT, (unit % LOAD_UNITS + 1) * UNIT)
-            grouped = stage.tile([P, PASSES, UNIT, PACK], BF16, align_bytes=64)
-            codes = packed.tile([P, PASSES, UNIT], U32, align_bytes=64)
-            scales = packed.tile([P, PASSES, UNIT], U8, align_bytes=64)
-            for g in range(PASSES):
-                src = raw[:, g, :, cols].rearrange("p j (c i) -> p c j i", i=4)
-                dst = grouped[:, g, :, :].rearrange("p (c i) j -> p c j i", i=4)
-                if unit < LOAD_UNITS and g > 0:
-                    nc.vector.tensor_copy(out=dst, in_=src)
-                else:
-                    nc.scalar.copy(out=dst, in_=src)
-            for g in range(PASSES):
-                for part in (slice(0, WIDE), slice(WIDE, UNIT)):
-                    nc.vector.quantize_mx(
-                        out=codes[:, g, part].bitcast(FP8X4),
-                        scales=scales[:, g, part],
-                        in_=grouped[:, g, part, :].rearrange("p w j -> p (w j)"),
-                    )
-            return codes, scales
+        w_codes = [None] * LOADS
+        w_scales = [None] * LOADS
+        w_grouped = [None] * PASSES
 
-        def multiply(codes, scales, b, e):
+        def regroup(load, g):
+            w_grouped[g] = stage.tile([P, LOAD_COLS, PACK], BF16, name="grouped", align_bytes=64)
+            src = w_raw[load][:, g, :, :].rearrange("p j (c i) -> p c j i", i=4)
+            dst = w_grouped[g][:].rearrange("p (c i) j -> p c j i", i=4)
+            if g == PASSES - 1 and (load == 0 or load >= ROPE_LOADS):
+                nc.vector.tensor_copy(out=dst, in_=src)
+            else:
+                nc.scalar.copy(out=dst, in_=src)
+
+        def quantise(load, g):
+            if g == 0:
+                w_codes[load] = packed.tile([P, PASSES, LOAD_COLS], U32, name="codes", align_bytes=64)
+                w_scales[load] = packed.tile([P, PASSES, LOAD_COLS], U8, name="scales", align_bytes=64)
+            for part in (slice(0, QUANT_COLS), slice(QUANT_COLS, LOAD_COLS)):
+                nc.vector.quantize_mx(
+                    out=w_codes[load][:, g, part].bitcast(FP8X4),
+                    scales=w_scales[load][:, g, part],
+                    in_=w_grouped[g][:, part, :].rearrange("p w j -> p (w j)"),
+                )
+
+        def multiply(unit, b, e):
+            codes = w_codes[unit // LOAD_UNITS]
+            scales = w_scales[unit // LOAD_UNITS]
+            first = (unit % LOAD_UNITS) * UNIT
             bank = psum.tile([P, BANK], F32, name="bank")
             tokens = slice(e * P, (e + 1) * P)
-            for part in (slice(0, WIDE), slice(WIDE, UNIT)):
+            for lo, hi in ((0, WIDE), (WIDE, UNIT)):
                 for g in range(PASSES):
                     nc.tensor.matmul_mx(
-                        out=bank[:, part],
+                        out=bank[:, lo:hi],
                         lhsT=x_codes[:, g, b, tokens].bitcast(FP8X4),
                         lhsT_scale=x_scales[:, g, b, tokens],
-                        rhs=codes[:, g, part].bitcast(FP8X4),
-                        rhs_scale=scales[:, g, part],
+                        rhs=codes[:, g, first + lo : first + hi].bitcast(FP8X4),
+                        rhs_scale=scales[:, g, first + lo : first + hi],
                         start=(g == 0),
                         stop=(g == PASSES - 1),
                     )
@@ -191,32 +198,37 @@ def tile_attention_pa_kernel(tc, x, f1, f2, f3, Wqkv, out_0, out_1, out_2):
                         ),
                         op=MULT,
                     )
-            nc.vector.tensor_tensor(out=rotated[:], in0=rotated[:], in1=crossed[:], op=ADD)
-
-        def finish(unit, codes, scales):
-            section = unit // UNITS_PER_SECTION
-            head = (unit % UNITS_PER_SECTION) * UNIT_HEADS
-            for b in range(BATCH):
-                banks = [multiply(codes, scales, b, e) for e in range(PAIR)]
-                done = result.tile([P, UNIT_HEADS, PAIR, HEAD_DIM], F32)
-                if section < ROPE_SECTIONS:
-                    rotate(banks, done)
-                else:
-                    for e in range(PAIR):
-                        nc.scalar.copy(
-                            out=done[:, :, e, :],
-                            in_=banks[e][:, 0:UNIT].rearrange("p (h d) -> p h d", h=UNIT_HEADS),
-                        )
-                nc.sync.dma_start(
-                    out=outs[section][b, head : head + UNIT_HEADS].rearrange(
-                        "h (p e) d -> p h (e d)", e=PAIR
-                    ),
-                    in_=done[:].rearrange("p h e d -> p h (e d)"),
+                nc.gpsimd.tensor_tensor(
+                    out=rotated[:, :, e, :], in0=rotated[:, :, e, :], in1=crossed[:, :, e, :], op=ADD
                 )
 
-        ready = [prepare(unit) for unit in range(AHEAD)]
-        for unit in range(UNITS):
-            if unit + AHEAD < UNITS:
-                ready.append(prepare(unit + AHEAD))
-            codes, scales = ready[unit]
-            finish(unit, codes, scales)
+        def finish(unit, b):
+            section = unit // UNITS_PER_SECTION
+            head = (unit % UNITS_PER_SECTION) * UNIT_HEADS
+            banks = [multiply(unit, b, e) for e in range(PAIR)]
+            done = result.tile([P, UNIT_HEADS, PAIR, HEAD_DIM], F32)
+            if section < ROPE_SECTIONS:
+                rotate(banks, done)
+            else:
+                plain = [bank[:, 0:UNIT].rearrange("p (h d) -> p h d", h=UNIT_HEADS) for bank in banks]
+                nc.scalar.copy(out=done[:, :, 0, :], in_=plain[0])
+                nc.vector.tensor_copy(out=done[:, :, 1, :], in_=plain[1])
+            nc.sync.dma_start(
+                out=outs[section][b, head : head + UNIT_HEADS].rearrange(
+                    "h (p e) d -> p h (e d)", e=PAIR
+                ),
+                in_=done[:].rearrange("p h e d -> p h (e d)"),
+            )
+
+        turn_x(0)
+        for g in range(PASSES):
+            regroup(0, g)
+        for g in range(PASSES):
+            quantise(0, g)
+        turn_x(1)
+        for load in range(LOADS):
+            for step in range(LOAD_UNITS * BATCH):
+                if step < PASSES and load + 1 < LOADS:
+                    regroup(load + 1, step)
+                    quantise(load + 1, step)
+                finish(load * LOAD_UNITS + step // BATCH, step % BATCH)

@@ -28,11 +28,11 @@ UNIT_HEADS = 4
 UNIT = UNIT_HEADS * HEAD_DIM
 WIDE = 256
 UNITS_PER_SECTION = HEADS // UNIT_HEADS
+UNITS = SECTIONS * UNITS_PER_SECTION
 LOAD_UNITS = 2
 LOAD_COLS = LOAD_UNITS * UNIT
-LOADS = SECTIONS * UNITS_PER_SECTION // LOAD_UNITS
-ROPE_LOADS = ROPE_SECTIONS * UNITS_PER_SECTION // LOAD_UNITS
-QUANT_COLS = 512
+LOADS = UNITS // LOAD_UNITS
+AHEAD = 2
 BANK = 512
 
 FLOPS = 2 * BATCH * TOKENS * DIM * SECTIONS * HEADS * HEAD_DIM
@@ -44,23 +44,20 @@ def tile_attention_pa_kernel(tc, x, f1, f2, f3, Wqkv, out_0, out_1, out_2):
 
     with ExitStack() as ctx:
         const = ctx.enter_context(tc.tile_pool(name="const", bufs=1))
-        stage = ctx.enter_context(tc.tile_pool(name="stage", bufs=4))
-        packed = ctx.enter_context(tc.tile_pool(name="packed", bufs=3))
-        result = ctx.enter_context(tc.tile_pool(name="result", bufs=6))
-        scratch = ctx.enter_context(tc.tile_pool(name="scratch", bufs=3))
+        fetched = ctx.enter_context(tc.tile_pool(name="fetched", bufs=3))
+        stage = ctx.enter_context(tc.tile_pool(name="stage", bufs=3))
+        packed = ctx.enter_context(tc.tile_pool(name="packed", bufs=4))
+        result = ctx.enter_context(tc.tile_pool(name="result", bufs=8))
         psum = ctx.enter_context(tc.psum_pool(name="psum", bufs=8))
-        ctx.enter_context(tc.manual_schedule())
 
         x_sb = const.tile([P, BATCH, PAIR * DIM], BF16)
-        w_raw = [
-            const.tile([P, PASSES, PACK, LOAD_COLS], BF16, name="w_raw%d" % load)
-            for load in range(LOADS)
-        ]
+        w_raw = {}
 
         def load_x(b):
             nc.sync.dma_start(out=x_sb[:, b, :], in_=x[b].rearrange("(p e) k -> p (e k)", e=PAIR))
 
         def load_weights(load):
+            w_raw[load] = fetched.tile([P, PASSES, PACK, LOAD_COLS], BF16, name="w_raw")
             cols = slice(load * LOAD_COLS, (load + 1) * LOAD_COLS)
             for g in range(PASSES):
                 rows = slice(g * K_PASS, (g + 1) * K_PASS)
@@ -69,33 +66,41 @@ def tile_attention_pa_kernel(tc, x, f1, f2, f3, Wqkv, out_0, out_1, out_2):
                     in_=Wqkv[rows, cols].rearrange("(p j) w -> p j w", j=PACK),
                 )
 
-        angles = const.tile([P, PAIR, AXES, 2 * HALF], BF16)
+        angles = const.tile([P, PAIR, AXES, 2, HALF], BF16)
         for axis, f in enumerate((f1, f2, f3)):
             nc.scalar.dma_start(
-                out=angles[:, :, axis, :], in_=f.rearrange("(p e) c -> p e c", e=PAIR)
+                out=angles[:, :, axis].rearrange("p e s i -> p e (s i)"),
+                in_=f.rearrange("(p e) c -> p e c", e=PAIR),
             )
 
+        order = []
+        for i in range(UNITS_PER_SECTION):
+            order.extend([2 * i, 2 * i + 1, ROPE_SECTIONS * UNITS_PER_SECTION + i])
+        load_order = []
+        for unit in order:
+            if unit // LOAD_UNITS not in load_order:
+                load_order.append(unit // LOAD_UNITS)
+
         load_x(0)
-        load_weights(0)
+        load_weights(load_order[0])
         load_x(1)
-        for load in range(1, LOADS):
+        for load in load_order[1:]:
             load_weights(load)
 
-        cos_t = const.tile([P, PAIR, AXES, 2, HALF], F32)
-        sin_t = const.tile([P, PAIR, AXES, 2, HALF], F32)
-        angle_halves = angles[:].rearrange("p e a (s i) -> p (e a) s i", s=2)
-        sin_halves = sin_t[:].rearrange("p e a s i -> p (e a) s i")
-        nc.scalar.activation(
-            out=cos_t[:].rearrange("p e a s i -> p (e a s i)"),
-            in_=angles[:].rearrange("p e a c -> p (e a c)"),
-            func=SIN,
-            scale=-1.0,
-            bias=math.pi / 2,
-        )
-        nc.scalar.activation(
-            out=sin_halves[:, :, 0, :], in_=angle_halves[:, :, 0, :], func=SIN, scale=-1.0
-        )
-        nc.scalar.activation(out=sin_halves[:, :, 1, :], in_=angle_halves[:, :, 1, :], func=SIN)
+        factors = const.tile([P, PAIR, 2, AXES, 2, HALF], F32)
+
+        def make_factors():
+            nc.scalar.activation(
+                out=factors[:, :, 0].rearrange("p e a s i -> p e (a s i)"),
+                in_=angles[:].rearrange("p e a s i -> p e (a s i)"),
+                func=SIN,
+                scale=-1.0,
+                bias=math.pi / 2,
+            )
+            nc.scalar.activation(out=factors[:, :, 1, :, 0, :], in_=angles[:, :, :, 1, :], func=SIN)
+            nc.scalar.activation(
+                out=factors[:, :, 1, :, 1, :], in_=angles[:, :, :, 0, :], func=SIN, scale=-1.0
+            )
 
         ident = const.tile([P, P], F32)
         make_identity(nc, ident[:])
@@ -130,105 +135,95 @@ def tile_attention_pa_kernel(tc, x, f1, f2, f3, Wqkv, out_0, out_1, out_2):
                     in_=x_grouped_cols[:, g, b, :],
                 )
 
-        w_codes = [None] * LOADS
-        w_scales = [None] * LOADS
-        w_grouped = [None] * PASSES
+        def prepare(unit):
+            raw = w_raw[unit // LOAD_UNITS]
+            cols = slice((unit % LOAD_UNITS) * UNIT, (unit % LOAD_UNITS + 1) * UNIT)
+            grouped = stage.tile([P, PASSES, UNIT, PACK], BF16, align_bytes=64)
+            codes = packed.tile([P, PASSES, UNIT], U32, align_bytes=64)
+            scales = packed.tile([P, PASSES, UNIT], U8, align_bytes=64)
+            for g in range(PASSES):
+                src = raw[:, g, :, cols].rearrange("p j (c i) -> p c j i", i=4)
+                dst = grouped[:, g, :, :].rearrange("p (c i) j -> p c j i", i=4)
+                if unit < LOAD_UNITS and g > 0:
+                    nc.vector.tensor_copy(out=dst, in_=src)
+                else:
+                    nc.scalar.copy(out=dst, in_=src)
+            for g in range(PASSES):
+                for part in (slice(0, WIDE), slice(WIDE, UNIT)):
+                    nc.vector.quantize_mx(
+                        out=codes[:, g, part].bitcast(FP8X4),
+                        scales=scales[:, g, part],
+                        in_=grouped[:, g, part, :].rearrange("p w j -> p (w j)"),
+                    )
+            return codes, scales
 
-        def regroup(load, g):
-            w_grouped[g] = stage.tile([P, LOAD_COLS, PACK], BF16, name="grouped", align_bytes=64)
-            src = w_raw[load][:, g, :, :].rearrange("p j (c i) -> p c j i", i=4)
-            dst = w_grouped[g][:].rearrange("p (c i) j -> p c j i", i=4)
-            if g == PASSES - 1 and (load == 0 or load >= ROPE_LOADS):
-                nc.vector.tensor_copy(out=dst, in_=src)
-            else:
-                nc.scalar.copy(out=dst, in_=src)
-
-        def quantise(load, g):
-            if g == 0:
-                w_codes[load] = packed.tile([P, PASSES, LOAD_COLS], U32, name="codes", align_bytes=64)
-                w_scales[load] = packed.tile([P, PASSES, LOAD_COLS], U8, name="scales", align_bytes=64)
-            for part in (slice(0, QUANT_COLS), slice(QUANT_COLS, LOAD_COLS)):
-                nc.vector.quantize_mx(
-                    out=w_codes[load][:, g, part].bitcast(FP8X4),
-                    scales=w_scales[load][:, g, part],
-                    in_=w_grouped[g][:, part, :].rearrange("p w j -> p (w j)"),
-                )
-
-        def multiply(unit, b, e):
-            codes = w_codes[unit // LOAD_UNITS]
-            scales = w_scales[unit // LOAD_UNITS]
-            first = (unit % LOAD_UNITS) * UNIT
+        def multiply(codes, scales, b, e):
             bank = psum.tile([P, BANK], F32, name="bank")
             tokens = slice(e * P, (e + 1) * P)
-            for lo, hi in ((0, WIDE), (WIDE, UNIT)):
+            for part in (slice(0, WIDE), slice(WIDE, UNIT)):
                 for g in range(PASSES):
                     nc.tensor.matmul_mx(
-                        out=bank[:, lo:hi],
+                        out=bank[:, part],
                         lhsT=x_codes[:, g, b, tokens].bitcast(FP8X4),
                         lhsT_scale=x_scales[:, g, b, tokens],
-                        rhs=codes[:, g, first + lo : first + hi].bitcast(FP8X4),
-                        rhs_scale=scales[:, g, first + lo : first + hi],
+                        rhs=codes[:, g, part].bitcast(FP8X4),
+                        rhs_scale=scales[:, g, part],
                         start=(g == 0),
                         stop=(g == PASSES - 1),
                     )
-            return bank
+            return bank[:, 0:UNIT].rearrange("p (h d) -> p h d", h=UNIT_HEADS)
 
-        def rotate(banks, rotated):
-            crossed = scratch.tile([P, UNIT_HEADS, PAIR, HEAD_DIM], F32)
+        def begin(unit, codes, scales, b):
+            banks = [multiply(codes, scales, b, e) for e in range(PAIR)]
+            scaled = result.tile([P, 2, UNIT_HEADS, PAIR, HEAD_DIM], F32)
+            shape = [P, 2, UNIT_HEADS, HEAD_DIM]
             for e in range(PAIR):
-                t = banks[e][:, 0:UNIT]
-                nc.vector.tensor_tensor(
-                    out=rotated[:, :, e, :],
-                    in0=t.rearrange("p (h d) -> p h d", h=UNIT_HEADS),
-                    in1=cos_t[:, e].rearrange("p a s i -> p (a s i)").unsqueeze(1).to_broadcast(
-                        [P, UNIT_HEADS, HEAD_DIM]
-                    ),
-                    op=MULT,
-                )
-                t_halves = t.rearrange("p (h a s i) -> p h a s i", h=UNIT_HEADS, a=AXES, s=2)
-                crossed_halves = crossed[:, :, e, :].rearrange(
-                    "p h (a s i) -> p h a s i", a=AXES, s=2
-                )
-                for s in range(2):
+                if unit // UNITS_PER_SECTION < ROPE_SECTIONS:
                     nc.vector.tensor_tensor(
-                        out=crossed_halves[:, :, :, s, :],
-                        in0=t_halves[:, :, :, 1 - s, :],
-                        in1=sin_t[:, e, :, s, :].unsqueeze(1).to_broadcast(
-                            [P, UNIT_HEADS, AXES, HALF]
-                        ),
+                        out=scaled[:, :, :, e, :],
+                        in0=banks[e].unsqueeze(1).to_broadcast(shape),
+                        in1=factors[:, e]
+                        .rearrange("p z a s i -> p z (a s i)")
+                        .unsqueeze(2)
+                        .to_broadcast(shape),
                         op=MULT,
                     )
-                nc.gpsimd.tensor_tensor(
-                    out=rotated[:, :, e, :], in0=rotated[:, :, e, :], in1=crossed[:, :, e, :], op=ADD
-                )
+                else:
+                    nc.scalar.copy(out=scaled[:, 0, :, e, :], in_=banks[e])
+            return unit, b, scaled
 
-        def finish(unit, b):
+        def end(unit, b, scaled):
             section = unit // UNITS_PER_SECTION
             head = (unit % UNITS_PER_SECTION) * UNIT_HEADS
-            banks = [multiply(unit, b, e) for e in range(PAIR)]
-            done = result.tile([P, UNIT_HEADS, PAIR, HEAD_DIM], F32)
             if section < ROPE_SECTIONS:
-                rotate(banks, done)
-            else:
-                plain = [bank[:, 0:UNIT].rearrange("p (h d) -> p h d", h=UNIT_HEADS) for bank in banks]
-                nc.scalar.copy(out=done[:, :, 0, :], in_=plain[0])
-                nc.vector.tensor_copy(out=done[:, :, 1, :], in_=plain[1])
+                halves = scaled[:].rearrange("p z h e (a s i) -> p z (h e) a s i", a=AXES, s=2)
+                for s in range(2):
+                    nc.vector.tensor_tensor(
+                        out=halves[:, 0, :, :, s, :],
+                        in0=halves[:, 0, :, :, s, :],
+                        in1=halves[:, 1, :, :, 1 - s, :],
+                        op=ADD,
+                    )
             nc.sync.dma_start(
                 out=outs[section][b, head : head + UNIT_HEADS].rearrange(
                     "h (p e) d -> p h (e d)", e=PAIR
                 ),
-                in_=done[:].rearrange("p h e d -> p h (e d)"),
+                in_=scaled[:, 0].rearrange("p h e d -> p h (e d)"),
             )
 
-        turn_x(0)
-        for g in range(PASSES):
-            regroup(0, g)
-        for g in range(PASSES):
-            quantise(0, g)
-        turn_x(1)
-        for load in range(LOADS):
-            for step in range(LOAD_UNITS * BATCH):
-                if step < PASSES and load + 1 < LOADS:
-                    regroup(load + 1, step)
-                    quantise(load + 1, step)
-                finish(load * LOAD_UNITS + step // BATCH, step % BATCH)
+        with tc.manual_schedule():
+            turn_x(0)
+            ready = [prepare(order[0])]
+            make_factors()
+            turn_x(1)
+            ready.append(prepare(order[1]))
+        begun = []
+        for n, unit in enumerate(order):
+            if n + AHEAD < UNITS:
+                ready.append(prepare(order[n + AHEAD]))
+            codes, scales = ready[n]
+            for b in range(BATCH):
+                begun.append(begin(unit, codes, scales, b))
+                if len(begun) > 1:
+                    end(*begun[-2])
+        end(*begun[-1])

@@ -44,27 +44,39 @@ def tile_attention_pa_kernel(tc, x, f1, f2, f3, Wqkv, out_0, out_1, out_2):
 
     with ExitStack() as ctx:
         const = ctx.enter_context(tc.tile_pool(name="const", bufs=1))
+        first = ctx.enter_context(tc.tile_pool(name="first", bufs=2))
         fetched = ctx.enter_context(tc.tile_pool(name="fetched", bufs=3))
         stage = ctx.enter_context(tc.tile_pool(name="stage", bufs=3))
         packed = ctx.enter_context(tc.tile_pool(name="packed", bufs=4))
-        result = ctx.enter_context(tc.tile_pool(name="result", bufs=8))
+        result = ctx.enter_context(tc.tile_pool(name="result", bufs=4))
         psum = ctx.enter_context(tc.psum_pool(name="psum", bufs=8))
 
+        order = []
+        for i in range(UNITS_PER_SECTION):
+            order.extend([2 * i, 2 * i + 1, ROPE_SECTIONS * UNITS_PER_SECTION + i])
+
+        def rotated(unit):
+            return unit // UNITS_PER_SECTION < ROPE_SECTIONS
+
         x_sb = const.tile([P, BATCH, PAIR * DIM], BF16)
-        w_raw = {}
+        raw_of = {}
 
         def load_x(b):
             nc.sync.dma_start(out=x_sb[:, b, :], in_=x[b].rearrange("(p e) k -> p (e k)", e=PAIR))
 
-        def load_weights(load):
-            w_raw[load] = fetched.tile([P, PASSES, PACK, LOAD_COLS], BF16, name="w_raw")
-            cols = slice(load * LOAD_COLS, (load + 1) * LOAD_COLS)
+        def load_weights(pool, units):
+            cols = len(units) * UNIT
+            w_raw = pool.tile([P, PASSES, PACK, cols], BF16, name="w_raw")
+            col0 = units[0] * UNIT
             for g in range(PASSES):
-                rows = slice(g * K_PASS, (g + 1) * K_PASS)
                 nc.sync.dma_start(
-                    out=w_raw[load][:, g, :, :],
-                    in_=Wqkv[rows, cols].rearrange("(p j) w -> p j w", j=PACK),
+                    out=w_raw[:, g, :, :],
+                    in_=Wqkv[g * K_PASS : (g + 1) * K_PASS, col0 : col0 + cols].rearrange(
+                        "(p j) w -> p j w", j=PACK
+                    ),
                 )
+            for i, unit in enumerate(units):
+                raw_of[unit] = (w_raw, i * UNIT)
 
         angles = const.tile([P, PAIR, AXES, 2, HALF], BF16)
         for axis, f in enumerate((f1, f2, f3)):
@@ -73,21 +85,20 @@ def tile_attention_pa_kernel(tc, x, f1, f2, f3, Wqkv, out_0, out_1, out_2):
                 in_=f.rearrange("(p e) c -> p e c", e=PAIR),
             )
 
-        order = []
-        for i in range(UNITS_PER_SECTION):
-            order.extend([2 * i, 2 * i + 1, ROPE_SECTIONS * UNITS_PER_SECTION + i])
-        load_order = []
-        for unit in order:
-            if unit // LOAD_UNITS not in load_order:
-                load_order.append(unit // LOAD_UNITS)
-
+        load_weights(first, [order[0]])
         load_x(0)
-        load_weights(load_order[0])
         load_x(1)
-        for load in load_order[1:]:
-            load_weights(load)
+        load_weights(first, [order[1]])
+        seen = [order[0], order[1]]
+        for unit in order:
+            if unit not in seen:
+                pair = [unit - unit % LOAD_UNITS, unit - unit % LOAD_UNITS + 1]
+                load_weights(fetched, pair)
+                seen.extend(pair)
 
         factors = const.tile([P, PAIR, 2, AXES, 2, HALF], F32)
+        warm = const.tile([P, 2], F32)
+        nc.gpsimd.memset(warm[:, 0:1], 0.0)
 
         def make_factors():
             nc.scalar.activation(
@@ -124,10 +135,12 @@ def tile_attention_pa_kernel(tc, x, f1, f2, f3, Wqkv, out_0, out_1, out_2):
                         nc.tensor.transpose(
                             turned_words[:, e, u, :], x_words[:, b, e, g, u, :], ident[:]
                         )
-                nc.vector.tensor_copy(
+                nc.scalar.copy(
                     out=x_grouped_words[:, g, b],
                     in_=turned_words.rearrange("p e u t -> p e t u"),
                 )
+
+        def quantise_x(b):
             for g in range(PASSES):
                 nc.vector.quantize_mx(
                     out=x_codes[:, g, b, :].bitcast(FP8X4),
@@ -135,95 +148,135 @@ def tile_attention_pa_kernel(tc, x, f1, f2, f3, Wqkv, out_0, out_1, out_2):
                     in_=x_grouped_cols[:, g, b, :],
                 )
 
-        def prepare(unit):
-            raw = w_raw[unit // LOAD_UNITS]
-            cols = slice((unit % LOAD_UNITS) * UNIT, (unit % LOAD_UNITS + 1) * UNIT)
-            grouped = stage.tile([P, PASSES, UNIT, PACK], BF16, align_bytes=64)
-            codes = packed.tile([P, PASSES, UNIT], U32, align_bytes=64)
-            scales = packed.tile([P, PASSES, UNIT], U8, align_bytes=64)
+        grouped_of = {}
+        packed_of = {}
+
+        def regroup(n, vector_passes):
+            raw, col0 = raw_of[order[n]]
+            grouped = stage.tile([P, PASSES, UNIT, PACK], BF16, align_bytes=64, name="grouped")
+            grouped_of[n] = grouped
             for g in range(PASSES):
-                src = raw[:, g, :, cols].rearrange("p j (c i) -> p c j i", i=4)
+                src = raw[:, g, :, col0 : col0 + UNIT].rearrange("p j (c i) -> p c j i", i=4)
                 dst = grouped[:, g, :, :].rearrange("p (c i) j -> p c j i", i=4)
-                if unit < LOAD_UNITS and g > 0:
+                if g in vector_passes:
                     nc.vector.tensor_copy(out=dst, in_=src)
                 else:
                     nc.scalar.copy(out=dst, in_=src)
-            for g in range(PASSES):
-                for part in (slice(0, WIDE), slice(WIDE, UNIT)):
-                    nc.vector.quantize_mx(
-                        out=codes[:, g, part].bitcast(FP8X4),
-                        scales=scales[:, g, part],
-                        in_=grouped[:, g, part, :].rearrange("p w j -> p (w j)"),
-                    )
-            return codes, scales
 
-        def multiply(codes, scales, b, e):
-            bank = psum.tile([P, BANK], F32, name="bank")
-            tokens = slice(e * P, (e + 1) * P)
-            for part in (slice(0, WIDE), slice(WIDE, UNIT)):
-                for g in range(PASSES):
-                    nc.tensor.matmul_mx(
-                        out=bank[:, part],
-                        lhsT=x_codes[:, g, b, tokens].bitcast(FP8X4),
-                        lhsT_scale=x_scales[:, g, b, tokens],
-                        rhs=codes[:, g, part].bitcast(FP8X4),
-                        rhs_scale=scales[:, g, part],
-                        start=(g == 0),
-                        stop=(g == PASSES - 1),
-                    )
-            return bank[:, 0:UNIT].rearrange("p (h d) -> p h d", h=UNIT_HEADS)
+        def quantise(n):
+            codes = packed.tile([P, PASSES * UNIT], U32, align_bytes=64, name="codes")
+            scales = packed.tile([P, PASSES * UNIT], U8, align_bytes=64, name="scales")
+            packed_of[n] = (codes, scales)
+            flat = grouped_of[n][:].rearrange("p g w j -> p (g w j)")
+            for part in (slice(0, 1024), slice(1024, PASSES * UNIT)):
+                nc.vector.quantize_mx(
+                    out=codes[:, part].bitcast(FP8X4),
+                    scales=scales[:, part],
+                    in_=flat[:, PACK * part.start : PACK * part.stop],
+                )
 
-        def begin(unit, codes, scales, b):
-            banks = [multiply(codes, scales, b, e) for e in range(PAIR)]
-            scaled = result.tile([P, 2, UNIT_HEADS, PAIR, HEAD_DIM], F32)
-            shape = [P, 2, UNIT_HEADS, HEAD_DIM]
+        banks_of = {}
+
+        def multiply(n, b):
+            codes, scales = packed_of[n]
             for e in range(PAIR):
-                if unit // UNITS_PER_SECTION < ROPE_SECTIONS:
+                bank = psum.tile([P, BANK], F32, name="bank")
+                tokens = slice(e * P, (e + 1) * P)
+                for part in (slice(0, WIDE), slice(WIDE, UNIT)):
+                    for g in range(PASSES):
+                        cols = slice(g * UNIT + part.start, g * UNIT + part.stop)
+                        nc.tensor.matmul_mx(
+                            out=bank[:, part],
+                            lhsT=x_codes[:, g, b, tokens].bitcast(FP8X4),
+                            lhsT_scale=x_scales[:, g, b, tokens],
+                            rhs=codes[:, cols].bitcast(FP8X4),
+                            rhs_scale=scales[:, cols],
+                            start=(g == 0),
+                            stop=(g == PASSES - 1),
+                        )
+                banks_of[(n, b, e)] = bank[:, 0:UNIT].rearrange("p (h d) -> p h d", h=UNIT_HEADS)
+
+        shape = [P, 2, UNIT_HEADS, HEAD_DIM]
+
+        def products(n, scaled):
+            for b in range(BATCH):
+                for e in range(PAIR):
                     nc.vector.tensor_tensor(
-                        out=scaled[:, :, :, e, :],
-                        in0=banks[e].unsqueeze(1).to_broadcast(shape),
+                        out=scaled[:, :, b, :, e, :],
+                        in0=banks_of[(n, b, e)].unsqueeze(1).to_broadcast(shape),
                         in1=factors[:, e]
                         .rearrange("p z a s i -> p z (a s i)")
                         .unsqueeze(2)
                         .to_broadcast(shape),
                         op=MULT,
                     )
-                else:
-                    nc.scalar.copy(out=scaled[:, 0, :, e, :], in_=banks[e])
-            return unit, b, scaled
 
-        def end(unit, b, scaled):
-            section = unit // UNITS_PER_SECTION
-            head = (unit % UNITS_PER_SECTION) * UNIT_HEADS
-            if section < ROPE_SECTIONS:
-                halves = scaled[:].rearrange("p z h e (a s i) -> p z (h e) a s i", a=AXES, s=2)
-                for s in range(2):
-                    nc.vector.tensor_tensor(
-                        out=halves[:, 0, :, :, s, :],
-                        in0=halves[:, 0, :, :, s, :],
-                        in1=halves[:, 1, :, :, 1 - s, :],
-                        op=ADD,
-                    )
-            nc.sync.dma_start(
-                out=outs[section][b, head : head + UNIT_HEADS].rearrange(
-                    "h (p e) d -> p h (e d)", e=PAIR
-                ),
-                in_=scaled[:, 0].rearrange("p h e d -> p h (e d)"),
+        def sums(engine, scaled, s, rows):
+            halves = scaled[:].rearrange("p z b h e (a s i) -> p z (b h e) a s i", a=AXES, s=2)
+            engine.tensor_tensor(
+                out=halves[:, 0, rows, :, s, :],
+                in0=halves[:, 0, rows, :, s, :],
+                in1=halves[:, 1, rows, :, 1 - s, :],
+                op=ADD,
             )
 
-        with tc.manual_schedule():
-            turn_x(0)
-            ready = [prepare(order[0])]
+        def store(n, scaled, b):
+            unit = order[n]
+            head = (unit % UNITS_PER_SECTION) * UNIT_HEADS
+            nc.sync.dma_start(
+                out=outs[unit // UNITS_PER_SECTION][b, head : head + UNIT_HEADS].rearrange(
+                    "h (p e) d -> p h (e d)", e=PAIR
+                ),
+                in_=scaled[:, 0, b].rearrange("p h e d -> p h (e d)"),
+            )
+
+        ROWS = BATCH * UNIT_HEADS * PAIR
+        every = slice(0, ROWS)
+        lower = slice(0, ROWS // 2)
+        upper = slice(ROWS // 2, ROWS)
+        fence = const.tile([P, 1], U32)
+
+        with tc.manual_schedule(engines={mybir.EngineType.DVE, mybir.EngineType.Pool, mybir.EngineType.Activation, mybir.EngineType.PE}):
+            nc.scalar.activation(out=warm[:, 1:2], in_=warm[:, 0:1], func=SIN)
             make_factors()
-            turn_x(1)
-            ready.append(prepare(order[1]))
-        begun = []
-        for n, unit in enumerate(order):
-            if n + AHEAD < UNITS:
-                ready.append(prepare(order[n + AHEAD]))
-            codes, scales = ready[n]
-            for b in range(BATCH):
-                begun.append(begin(unit, codes, scales, b))
-                if len(begun) > 1:
-                    end(*begun[-2])
-        end(*begun[-1])
+            pending = []
+            for n in range(-2, UNITS):
+                if n == -1:
+                    turn_x(0)
+                    quantise_x(0)
+                    turn_x(1)
+                    quantise_x(1)
+                if 0 <= n + 1 < UNITS:
+                    quantise(n + 1)
+                    for b in range(BATCH):
+                        multiply(n + 1, b)
+                if n >= 0 and rotated(order[n]):
+                    scaled = result.tile(
+                        [P, 2, BATCH, UNIT_HEADS, PAIR, HEAD_DIM], F32, name="scaled"
+                    )
+                    if pending:
+                        if n + 1 < UNITS:
+                            nc.gpsimd.tensor_copy(out=fence[:], in_=packed_of[n + 1][0][:, 1024:1025])
+                        sums(nc.gpsimd, pending[1], 0, every)
+                        sums(nc.gpsimd, pending[1], 1, lower)
+                    products(n, scaled)
+                    if pending:
+                        sums(nc.vector, pending[1], 1, upper)
+                        for b in range(BATCH):
+                            store(pending[0], pending[1], b)
+                    pending = [n, scaled]
+                elif n >= 0:
+                    scaled = result.tile(
+                        [P, 1, BATCH, UNIT_HEADS, PAIR, HEAD_DIM], F32, name="scaled"
+                    )
+                    for b in range(BATCH):
+                        for e in range(PAIR):
+                            nc.scalar.copy(out=scaled[:, 0, b, :, e, :], in_=banks_of[(n, b, e)])
+                        store(n, scaled, b)
+                if n + 2 < UNITS:
+                    regroup(n + 2, (1, 2) if n < 0 or not rotated(order[n]) else ())
+                if n == UNITS - 2:
+                    for rows, b in ((lower, 0), (upper, 1)):
+                        for s in range(2):
+                            sums(nc.vector, pending[1], s, rows)
+                        store(pending[0], pending[1], b)

@@ -44,30 +44,31 @@ def tile_attention_pa_kernel(tc, x, f1, f2, f3, Wqkv, out_0, out_1, out_2):
 
     with ExitStack() as ctx:
         const = ctx.enter_context(tc.tile_pool(name="const", bufs=1))
-        first = ctx.enter_context(tc.tile_pool(name="first", bufs=2))
-        fetched = ctx.enter_context(tc.tile_pool(name="fetched", bufs=3))
+        single = ctx.enter_context(tc.tile_pool(name="single", bufs=2))
+        double = ctx.enter_context(tc.tile_pool(name="double", bufs=1))
+        fetched = ctx.enter_context(tc.tile_pool(name="fetched", bufs=2))
         stage = ctx.enter_context(tc.tile_pool(name="stage", bufs=3))
         packed = ctx.enter_context(tc.tile_pool(name="packed", bufs=4))
         result = ctx.enter_context(tc.tile_pool(name="result", bufs=4))
         psum = ctx.enter_context(tc.psum_pool(name="psum", bufs=8))
 
-        order = []
-        for i in range(UNITS_PER_SECTION):
-            order.extend([2 * i, 2 * i + 1, ROPE_SECTIONS * UNITS_PER_SECTION + i])
+        order = list(range(UNITS))
 
         def rotated(unit):
             return unit // UNITS_PER_SECTION < ROPE_SECTIONS
 
-        x_sb = const.tile([P, BATCH, PAIR * DIM], BF16)
+        x_sb = result.tile([P, BATCH, PAIR * DIM], BF16, align_bytes=64, name="scaled")
         raw_of = {}
 
         def load_x(b):
             nc.sync.dma_start(out=x_sb[:, b, :], in_=x[b].rearrange("(p e) k -> p (e k)", e=PAIR))
 
-        def load_weights(pool, units):
+        pool_of = {1: single, 2: double, 4: fetched}
+
+        def load_weights(units):
             cols = len(units) * UNIT
-            w_raw = pool.tile([P, PASSES, PACK, cols], BF16, name="w_raw")
             col0 = units[0] * UNIT
+            w_raw = pool_of[len(units)].tile([P, PASSES, PACK, cols], BF16, name="w_raw")
             for g in range(PASSES):
                 nc.sync.dma_start(
                     out=w_raw[:, g, :, :],
@@ -85,16 +86,12 @@ def tile_attention_pa_kernel(tc, x, f1, f2, f3, Wqkv, out_0, out_1, out_2):
                 in_=f.rearrange("(p e) c -> p e c", e=PAIR),
             )
 
-        load_weights(first, [order[0]])
+        load_weights([0])
         load_x(0)
         load_x(1)
-        load_weights(first, [order[1]])
-        seen = [order[0], order[1]]
-        for unit in order:
-            if unit not in seen:
-                pair = [unit - unit % LOAD_UNITS, unit - unit % LOAD_UNITS + 1]
-                load_weights(fetched, pair)
-                seen.extend(pair)
+        load_weights([1])
+        load_weights([2, 3])
+        load_weights([4, 5, 6, 7])
 
         factors = const.tile([P, PAIR, 2, AXES, 2, HALF], F32)
         warm = const.tile([P, 2], F32)
@@ -118,7 +115,9 @@ def tile_attention_pa_kernel(tc, x, f1, f2, f3, Wqkv, out_0, out_1, out_2):
         x_words = x_sb[:].bitcast(F32).rearrange(
             "p b (e g q u) -> p b e g u q", e=PAIR, g=PASSES, u=2
         )
-        x_grouped = const.tile([P, PASSES * BATCH * PAIR * P * PACK], BF16, align_bytes=64)
+        x_grouped = result.tile(
+            [P, PASSES * BATCH * PAIR * P * PACK], BF16, align_bytes=64, name="scaled"
+        )
         x_grouped_words = x_grouped[:].bitcast(F32).rearrange(
             "p (g b e t u) -> p g b e t u", g=PASSES, b=BATCH, e=PAIR, u=2
         )
@@ -236,7 +235,7 @@ def tile_attention_pa_kernel(tc, x, f1, f2, f3, Wqkv, out_0, out_1, out_2):
         upper = slice(ROWS // 2, ROWS)
         fence = const.tile([P, 1], U32)
 
-        with tc.manual_schedule(engines={mybir.EngineType.DVE, mybir.EngineType.Pool, mybir.EngineType.Activation, mybir.EngineType.PE}):
+        with tc.manual_schedule():
             nc.scalar.activation(out=warm[:, 1:2], in_=warm[:, 0:1], func=SIN)
             make_factors()
             pending = []
@@ -252,7 +251,7 @@ def tile_attention_pa_kernel(tc, x, f1, f2, f3, Wqkv, out_0, out_1, out_2):
                         multiply(n + 1, b)
                 if n >= 0 and rotated(order[n]):
                     scaled = result.tile(
-                        [P, 2, BATCH, UNIT_HEADS, PAIR, HEAD_DIM], F32, name="scaled"
+                        [P, 2, BATCH, UNIT_HEADS, PAIR, HEAD_DIM], F32, align_bytes=64, name="scaled"
                     )
                     if pending:
                         if n + 1 < UNITS:
@@ -267,15 +266,17 @@ def tile_attention_pa_kernel(tc, x, f1, f2, f3, Wqkv, out_0, out_1, out_2):
                     pending = [n, scaled]
                 elif n >= 0:
                     scaled = result.tile(
-                        [P, 1, BATCH, UNIT_HEADS, PAIR, HEAD_DIM], F32, name="scaled"
+                        [P, 1, BATCH, UNIT_HEADS, PAIR, HEAD_DIM], F32, align_bytes=64, name="scaled"
                     )
                     for b in range(BATCH):
                         for e in range(PAIR):
                             nc.scalar.copy(out=scaled[:, 0, b, :, e, :], in_=banks_of[(n, b, e)])
                         store(n, scaled, b)
+                if n == 2:
+                    load_weights([8, 9, 10, 11])
                 if n + 2 < UNITS:
                     regroup(n + 2, (1, 2) if n < 0 or not rotated(order[n]) else ())
-                if n == UNITS - 2:
+                if n == ROPE_SECTIONS * UNITS_PER_SECTION - 1:
                     for rows, b in ((lower, 0), (upper, 1)):
                         for s in range(2):
                             sums(nc.vector, pending[1], s, rows)

@@ -60,8 +60,12 @@ def tile_attention_pa_kernel(tc, x, f1, f2, f3, Wqkv, out_0, out_1, out_2):
         x_sb = result.tile([P, BATCH, PAIR * DIM], BF16, align_bytes=64, name="scaled")
         raw_of = {}
 
-        def load_x(b):
-            nc.sync.dma_start(out=x_sb[:, b, :], in_=x[b].rearrange("(p e) k -> p (e k)", e=PAIR))
+        def load_x(c):
+            for b in range(BATCH):
+                nc.sync.dma_start(
+                    out=x_sb[b:P:BATCH, c, :],
+                    in_=x[b].rearrange("(m c f) k -> m c (f k)", c=2, f=PAIR)[:, c, :],
+                )
 
         pool_of = {1: single, 2: double, 4: fetched}
 
@@ -79,35 +83,38 @@ def tile_attention_pa_kernel(tc, x, f1, f2, f3, Wqkv, out_0, out_1, out_2):
             for i, unit in enumerate(units):
                 raw_of[unit] = (w_raw, i * UNIT)
 
-        angles = const.tile([P, PAIR, AXES, 2, HALF], BF16)
-        for axis, f in enumerate((f1, f2, f3)):
-            nc.scalar.dma_start(
-                out=angles[:, :, axis].rearrange("p e s i -> p e (s i)"),
-                in_=f.rearrange("(p e) c -> p e c", e=PAIR),
-            )
+        angles = const.tile([P, AXES, BATCH * PAIR, 2 * HALF], BF16)
 
         load_weights([0])
         load_x(0)
         load_x(1)
         load_weights([1])
+        for axis, f in enumerate((f1, f2, f3)):
+            for b in range(BATCH):
+                nc.sync.dma_start(
+                    out=angles[b:P:BATCH, axis].rearrange("p t c -> p (t c)"),
+                    in_=f.rearrange("(m t) c -> m (t c)", t=BATCH * PAIR),
+                )
         load_weights([2, 3])
         load_weights([4, 5, 6, 7])
 
-        factors = const.tile([P, PAIR, 2, AXES, 2, HALF], F32)
+        factors = const.tile([P, BATCH, PAIR, 2, AXES, 2, HALF], F32)
         warm = const.tile([P, 2], F32)
         nc.gpsimd.memset(warm[:, 0:1], 0.0)
 
         def make_factors():
+            by_token = factors[:].rearrange("p c e z a s i -> p (c e) z a s i")
+            halves = angles[:].rearrange("p a t (s i) -> p t a s i", s=2)
             nc.scalar.activation(
-                out=factors[:, :, 0].rearrange("p e a s i -> p e (a s i)"),
-                in_=angles[:].rearrange("p e a s i -> p e (a s i)"),
+                out=by_token[:, :, 0].rearrange("p t a s i -> p t a (s i)"),
+                in_=angles[:].rearrange("p a t c -> p t a c"),
                 func=SIN,
                 scale=-1.0,
                 bias=math.pi / 2,
             )
-            nc.scalar.activation(out=factors[:, :, 1, :, 0, :], in_=angles[:, :, :, 1, :], func=SIN)
+            nc.scalar.activation(out=by_token[:, :, 1, :, 0, :], in_=halves[:, :, :, 1, :], func=SIN)
             nc.scalar.activation(
-                out=factors[:, :, 1, :, 1, :], in_=angles[:, :, :, 0, :], func=SIN, scale=-1.0
+                out=by_token[:, :, 1, :, 1, :], in_=halves[:, :, :, 0, :], func=SIN, scale=-1.0
             )
 
         ident = const.tile([P, P], F32)
@@ -201,9 +208,9 @@ def tile_attention_pa_kernel(tc, x, f1, f2, f3, Wqkv, out_0, out_1, out_2):
             for b in range(BATCH):
                 for e in range(PAIR):
                     nc.vector.tensor_tensor(
-                        out=scaled[:, :, b, :, e, :],
+                        out=scaled[:, :, :, b, e, :],
                         in0=banks_of[(n, b, e)].unsqueeze(1).to_broadcast(shape),
-                        in1=factors[:, e]
+                        in1=factors[:, b, e]
                         .rearrange("p z a s i -> p z (a s i)")
                         .unsqueeze(2)
                         .to_broadcast(shape),
@@ -211,7 +218,7 @@ def tile_attention_pa_kernel(tc, x, f1, f2, f3, Wqkv, out_0, out_1, out_2):
                     )
 
         def sums(engine, scaled, s, rows):
-            halves = scaled[:].rearrange("p z b h e (a s i) -> p z (b h e) a s i", a=AXES, s=2)
+            halves = scaled[:].rearrange("p z h c e (a s i) -> p z (h c e) a s i", a=AXES, s=2)
             engine.tensor_tensor(
                 out=halves[:, 0, rows, :, s, :],
                 in0=halves[:, 0, rows, :, s, :],
@@ -224,9 +231,9 @@ def tile_attention_pa_kernel(tc, x, f1, f2, f3, Wqkv, out_0, out_1, out_2):
             head = (unit % UNITS_PER_SECTION) * UNIT_HEADS
             nc.sync.dma_start(
                 out=outs[unit // UNITS_PER_SECTION][b, head : head + UNIT_HEADS].rearrange(
-                    "h (p e) d -> p h (e d)", e=PAIR
+                    "h (m t) d -> m h (t d)", t=BATCH * PAIR
                 ),
-                in_=scaled[:, 0, b].rearrange("p h e d -> p h (e d)"),
+                in_=scaled[b:P:BATCH, 0].rearrange("p h c e d -> p h (c e d)"),
             )
 
         ROWS = BATCH * UNIT_HEADS * PAIR
@@ -237,7 +244,6 @@ def tile_attention_pa_kernel(tc, x, f1, f2, f3, Wqkv, out_0, out_1, out_2):
 
         with tc.manual_schedule():
             nc.scalar.activation(out=warm[:, 1:2], in_=warm[:, 0:1], func=SIN)
-            make_factors()
             pending = []
             for n in range(-2, UNITS):
                 if n == -1:
@@ -251,7 +257,7 @@ def tile_attention_pa_kernel(tc, x, f1, f2, f3, Wqkv, out_0, out_1, out_2):
                         multiply(n + 1, b)
                 if n >= 0 and rotated(order[n]):
                     scaled = result.tile(
-                        [P, 2, BATCH, UNIT_HEADS, PAIR, HEAD_DIM], F32, align_bytes=64, name="scaled"
+                        [P, 2, UNIT_HEADS, BATCH, PAIR, HEAD_DIM], F32, align_bytes=64, name="scaled"
                     )
                     if pending:
                         if n + 1 < UNITS:
@@ -266,18 +272,21 @@ def tile_attention_pa_kernel(tc, x, f1, f2, f3, Wqkv, out_0, out_1, out_2):
                     pending = [n, scaled]
                 elif n >= 0:
                     scaled = result.tile(
-                        [P, 1, BATCH, UNIT_HEADS, PAIR, HEAD_DIM], F32, align_bytes=64, name="scaled"
+                        [P, 1, UNIT_HEADS, BATCH, PAIR, HEAD_DIM], F32, align_bytes=64, name="scaled"
                     )
                     for b in range(BATCH):
                         for e in range(PAIR):
-                            nc.scalar.copy(out=scaled[:, 0, b, :, e, :], in_=banks_of[(n, b, e)])
+                            nc.scalar.copy(out=scaled[:, 0, :, b, e, :], in_=banks_of[(n, b, e)])
+                    for b in range(BATCH):
                         store(n, scaled, b)
                 if n == 2:
                     load_weights([8, 9, 10, 11])
                 if n + 2 < UNITS:
                     regroup(n + 2, (1, 2) if n < 0 or not rotated(order[n]) else ())
+                if n == -1:
+                    make_factors()
                 if n == ROPE_SECTIONS * UNITS_PER_SECTION - 1:
-                    for rows, b in ((lower, 0), (upper, 1)):
-                        for s in range(2):
-                            sums(nc.vector, pending[1], s, rows)
+                    for s in range(2):
+                        sums(nc.vector, pending[1], s, every)
+                    for b in range(BATCH):
                         store(pending[0], pending[1], b)

@@ -57,13 +57,15 @@ def tile_attention_pa_kernel(tc, x, f1, f2, f3, Wqkv, out_0, out_1, out_2):
         def rotated(unit):
             return unit // UNITS_PER_SECTION < ROPE_SECTIONS
 
-        x_sb = result.tile([P, BATCH, PAIR * DIM], BF16, align_bytes=64, name="scaled")
+        x_sb = [
+            result.tile([P, PAIR * DIM], BF16, align_bytes=64, name="scaled") for c in range(2)
+        ]
         raw_of = {}
 
         def load_x(c):
             for b in range(BATCH):
                 nc.sync.dma_start(
-                    out=x_sb[b:P:BATCH, c, :],
+                    out=x_sb[c][b:P:BATCH, :],
                     in_=x[b].rearrange("(m c f) k -> m c (f k)", c=2, f=PAIR)[:, c, :],
                 )
 
@@ -119,9 +121,10 @@ def tile_attention_pa_kernel(tc, x, f1, f2, f3, Wqkv, out_0, out_1, out_2):
 
         ident = const.tile([P, P], F32)
         make_identity(nc, ident[:])
-        x_words = x_sb[:].bitcast(F32).rearrange(
-            "p b (e g q u) -> p b e g u q", e=PAIR, g=PASSES, u=2
-        )
+        x_words = [
+            x_sb[c][:].bitcast(F32).rearrange("p (e g q u) -> p e g u q", e=PAIR, g=PASSES, u=2)
+            for c in range(2)
+        ]
         x_grouped = result.tile(
             [P, PASSES * BATCH * PAIR * P * PACK], BF16, align_bytes=64, name="scaled"
         )
@@ -139,7 +142,7 @@ def tile_attention_pa_kernel(tc, x, f1, f2, f3, Wqkv, out_0, out_1, out_2):
                 for e in range(PAIR):
                     for u in range(2):
                         nc.tensor.transpose(
-                            turned_words[:, e, u, :], x_words[:, b, e, g, u, :], ident[:]
+                            turned_words[:, e, u, :], x_words[b][:, e, g, u, :], ident[:]
                         )
                 nc.scalar.copy(
                     out=x_grouped_words[:, g, b],
@@ -236,6 +239,16 @@ def tile_attention_pa_kernel(tc, x, f1, f2, f3, Wqkv, out_0, out_1, out_2):
                 in_=scaled[b:P:BATCH, 0].rearrange("p h c e d -> p h (c e d)"),
             )
 
+        def store_half(n, scaled, b, c):
+            unit = order[n]
+            head = (unit % UNITS_PER_SECTION) * UNIT_HEADS
+            nc.sync.dma_start(
+                out=outs[unit // UNITS_PER_SECTION][b, head : head + UNIT_HEADS].rearrange(
+                    "h (m c f) d -> m h c (f d)", c=2, f=PAIR
+                )[:, :, c, :],
+                in_=scaled[b:P:BATCH, 0, :, c].rearrange("p h e d -> p h (e d)"),
+            )
+
         ROWS = BATCH * UNIT_HEADS * PAIR
         every = slice(0, ROWS)
         lower = slice(0, ROWS // 2)
@@ -274,11 +287,15 @@ def tile_attention_pa_kernel(tc, x, f1, f2, f3, Wqkv, out_0, out_1, out_2):
                     scaled = result.tile(
                         [P, 1, UNIT_HEADS, BATCH, PAIR, HEAD_DIM], F32, align_bytes=64, name="scaled"
                     )
-                    for b in range(BATCH):
+                    for c in range(2):
                         for e in range(PAIR):
-                            nc.scalar.copy(out=scaled[:, 0, :, b, e, :], in_=banks_of[(n, b, e)])
-                    for b in range(BATCH):
-                        store(n, scaled, b)
+                            nc.scalar.copy(out=scaled[:, 0, :, c, e, :], in_=banks_of[(n, c, e)])
+                        if n == UNITS - 1:
+                            for b in range(BATCH):
+                                store_half(n, scaled, b, c)
+                    if n < UNITS - 1:
+                        for b in range(BATCH):
+                            store(n, scaled, b)
                 if n == 2:
                     load_weights([8, 9, 10, 11])
                 if n + 2 < UNITS:

import math
from contextlib import ExitStack

import concourse.mybir as mybir
from concourse.masks import make_identity

F32 = mybir.dt.float32
BF16 = mybir.dt.bfloat16
U32 = mybir.dt.uint32
U8 = mybir.dt.uint8
FP8X4 = mybir.dt.float8_e4m3fn_x4
MULT = mybir.AluOpType.mult
ADD = mybir.AluOpType.add
SIN = mybir.ActivationFunctionType.Sin

BATCH, TOKENS, DIM, HEADS, HEAD_DIM = 2, 256, 1536, 16, 96
SECTIONS = 3
ROPE_SECTIONS = 2
AXES, HALF = 3, 16

P = 128
PACK = 4
K_PASS = P * PACK
PASSES = DIM // K_PASS
PAIR = TOKENS // P

UNIT_HEADS = 4
UNIT = UNIT_HEADS * HEAD_DIM
WIDE = 256
UNITS_PER_SECTION = HEADS // UNIT_HEADS
UNITS = SECTIONS * UNITS_PER_SECTION
LOAD_UNITS = 2
LOAD_COLS = LOAD_UNITS * UNIT
LOADS = UNITS // LOAD_UNITS
AHEAD = 2
BANK = 512

FLOPS = 2 * BATCH * TOKENS * DIM * SECTIONS * HEADS * HEAD_DIM


def tile_attention_pa_kernel(tc, x, f1, f2, f3, Wqkv, out_0, out_1, out_2):
    nc = tc.nc
    outs = (out_0, out_1, out_2)

    with ExitStack() as ctx:
        const = ctx.enter_context(tc.tile_pool(name="const", bufs=1))
        single = ctx.enter_context(tc.tile_pool(name="single", bufs=2))
        double = ctx.enter_context(tc.tile_pool(name="double", bufs=1))
        fetched = ctx.enter_context(tc.tile_pool(name="fetched", bufs=2))
        stage = ctx.enter_context(tc.tile_pool(name="stage", bufs=3))
        packed = ctx.enter_context(tc.tile_pool(name="packed", bufs=4))
        result = ctx.enter_context(tc.tile_pool(name="result", bufs=4))
        psum = ctx.enter_context(tc.psum_pool(name="psum", bufs=8))

        order = list(range(UNITS))

        def rotated(unit):
            return unit // UNITS_PER_SECTION < ROPE_SECTIONS

        x_sb = [
            result.tile([P, PAIR * DIM], BF16, align_bytes=64, name="scaled") for c in range(2)
        ]
        raw_of = {}

        def load_x(c):
            for b in range(BATCH):
                nc.sync.dma_start(
                    out=x_sb[c][b:P:BATCH, :],
                    in_=x[b].rearrange("(m c f) k -> m c (f k)", c=2, f=PAIR)[:, c, :],
                )

        pool_of = {1: single, 2: double, 4: fetched}

        def load_weights(units):
            cols = len(units) * UNIT
            col0 = units[0] * UNIT
            w_raw = pool_of[len(units)].tile([P, PASSES, PACK, cols], BF16, name="w_raw")
            for g in range(PASSES):
                nc.sync.dma_start(
                    out=w_raw[:, g, :, :],
                    in_=Wqkv[g * K_PASS : (g + 1) * K_PASS, col0 : col0 + cols].rearrange(
                        "(p j) w -> p j w", j=PACK
                    ),
                )
            for i, unit in enumerate(units):
                raw_of[unit] = (w_raw, i * UNIT)

        angles = const.tile([P, AXES, BATCH * PAIR, 2 * HALF], BF16)

        load_weights([0])
        load_x(0)
        load_x(1)
        load_weights([1])
        for axis, f in enumerate((f1, f2, f3)):
            for b in range(BATCH):
                nc.sync.dma_start(
                    out=angles[b:P:BATCH, axis].rearrange("p t c -> p (t c)"),
                    in_=f.rearrange("(m t) c -> m (t c)", t=BATCH * PAIR),
                )
        load_weights([2, 3])
        load_weights([4, 5, 6, 7])

        factors = const.tile([P, BATCH, PAIR, 2, AXES, 2, HALF], F32)
        warm = const.tile([P, 2], F32)
        nc.gpsimd.memset(warm[:, 0:1], 0.0)

        def make_factors():
            by_token = factors[:].rearrange("p c e z a s i -> p (c e) z a s i")
            halves = angles[:].rearrange("p a t (s i) -> p t a s i", s=2)
            nc.scalar.activation(
                out=by_token[:, :, 0].rearrange("p t a s i -> p t a (s i)"),
                in_=angles[:].rearrange("p a t c -> p t a c"),
                func=SIN,
                scale=-1.0,
                bias=math.pi / 2,
            )
            nc.scalar.activation(out=by_token[:, :, 1, :, 0, :], in_=halves[:, :, :, 1, :], func=SIN)
            nc.scalar.activation(
                out=by_token[:, :, 1, :, 1, :], in_=halves[:, :, :, 0, :], func=SIN, scale=-1.0
            )

        ident = const.tile([P, P], F32)
        make_identity(nc, ident[:])
        x_words = [
            x_sb[c][:].bitcast(F32).rearrange("p (e g q u) -> p e g u q", e=PAIR, g=PASSES, u=2)
            for c in range(2)
        ]
        x_grouped = result.tile(
            [P, PASSES * BATCH * PAIR * P * PACK], BF16, align_bytes=64, name="scaled"
        )
        x_grouped_words = x_grouped[:].bitcast(F32).rearrange(
            "p (g b e t u) -> p g b e t u", g=PASSES, b=BATCH, e=PAIR, u=2
        )
        x_grouped_cols = x_grouped[:].rearrange("p (g b c) -> p g b c", g=PASSES, b=BATCH)
        x_codes = const.tile([P, PASSES, BATCH, PAIR * P], U32, align_bytes=64)
        x_scales = const.tile([P, PASSES, BATCH, PAIR * P], U8, align_bytes=64)

        def turn_x(b):
            for g in range(PASSES):
                turned = psum.tile([P, BANK], F32, name="bank")
                turned_words = turned[:].rearrange("p (e u t) -> p e u t", e=PAIR, u=2)
                for e in range(PAIR):
                    for u in range(2):
                        nc.tensor.transpose(
                            turned_words[:, e, u, :], x_words[b][:, e, g, u, :], ident[:]
                        )
                nc.scalar.copy(
                    out=x_grouped_words[:, g, b],
                    in_=turned_words.rearrange("p e u t -> p e t u"),
                )

        def quantise_x(b):
            for g in range(PASSES):
                nc.vector.quantize_mx(
                    out=x_codes[:, g, b, :].bitcast(FP8X4),
                    scales=x_scales[:, g, b, :],
                    in_=x_grouped_cols[:, g, b, :],
                )

        grouped_of = {}
        packed_of = {}

        def regroup(n, vector_passes):
            raw, col0 = raw_of[order[n]]
            grouped = stage.tile([P, PASSES, UNIT, PACK], BF16, align_bytes=64, name="grouped")
            grouped_of[n] = grouped
            for g in range(PASSES):
                src = raw[:, g, :, col0 : col0 + UNIT].rearrange("p j (c i) -> p c j i", i=4)
                dst = grouped[:, g, :, :].rearrange("p (c i) j -> p c j i", i=4)
                if g in vector_passes:
                    nc.vector.tensor_copy(out=dst, in_=src)
                else:
                    nc.scalar.copy(out=dst, in_=src)

        def quantise(n):
            codes = packed.tile([P, PASSES * UNIT], U32, align_bytes=64, name="codes")
            scales = packed.tile([P, PASSES * UNIT], U8, align_bytes=64, name="scales")
            packed_of[n] = (codes, scales)
            flat = grouped_of[n][:].rearrange("p g w j -> p (g w j)")
            for part in (slice(0, 1024), slice(1024, PASSES * UNIT)):
                nc.vector.quantize_mx(
                    out=codes[:, part].bitcast(FP8X4),
                    scales=scales[:, part],
                    in_=flat[:, PACK * part.start : PACK * part.stop],
                )

        banks_of = {}

        def multiply(n, b):
            codes, scales = packed_of[n]
            for e in range(PAIR):
                bank = psum.tile([P, BANK], F32, name="bank")
                tokens = slice(e * P, (e + 1) * P)
                for part in (slice(0, WIDE), slice(WIDE, UNIT)):
                    for g in range(PASSES):
                        cols = slice(g * UNIT + part.start, g * UNIT + part.stop)
                        nc.tensor.matmul_mx(
                            out=bank[:, part],
                            lhsT=x_codes[:, g, b, tokens].bitcast(FP8X4),
                            lhsT_scale=x_scales[:, g, b, tokens],
                            rhs=codes[:, cols].bitcast(FP8X4),
                            rhs_scale=scales[:, cols],
                            start=(g == 0),
                            stop=(g == PASSES - 1),
                        )
                banks_of[(n, b, e)] = bank[:, 0:UNIT].rearrange("p (h d) -> p h d", h=UNIT_HEADS)

        shape = [P, 2, UNIT_HEADS, HEAD_DIM]

        def products(n, scaled):
            for b in range(BATCH):
                for e in range(PAIR):
                    nc.vector.tensor_tensor(
                        out=scaled[:, :, :, b, e, :],
                        in0=banks_of[(n, b, e)].unsqueeze(1).to_broadcast(shape),
                        in1=factors[:, b, e]
                        .rearrange("p z a s i -> p z (a s i)")
                        .unsqueeze(2)
                        .to_broadcast(shape),
                        op=MULT,
                    )

        def sums(engine, scaled, s, rows):
            halves = scaled[:].rearrange("p z h c e (a s i) -> p z (h c e) a s i", a=AXES, s=2)
            engine.tensor_tensor(
                out=halves[:, 0, rows, :, s, :],
                in0=halves[:, 0, rows, :, s, :],
                in1=halves[:, 1, rows, :, 1 - s, :],
                op=ADD,
            )

        def store(n, scaled, b):
            unit = order[n]
            head = (unit % UNITS_PER_SECTION) * UNIT_HEADS
            nc.sync.dma_start(
                out=outs[unit // UNITS_PER_SECTION][b, head : head + UNIT_HEADS].rearrange(
                    "h (m t) d -> m h (t d)", t=BATCH * PAIR
                ),
                in_=scaled[b:P:BATCH, 0].rearrange("p h c e d -> p h (c e d)"),
            )

        def store_half(n, scaled, b, c):
            unit = order[n]
            head = (unit % UNITS_PER_SECTION) * UNIT_HEADS
            nc.sync.dma_start(
                out=outs[unit // UNITS_PER_SECTION][b, head : head + UNIT_HEADS].rearrange(
                    "h (m c f) d -> m h c (f d)", c=2, f=PAIR
                )[:, :, c, :],
                in_=scaled[b:P:BATCH, 0, :, c].rearrange("p h e d -> p h (e d)"),
            )

        ROWS = BATCH * UNIT_HEADS * PAIR
        every = slice(0, ROWS)
        lower = slice(0, ROWS // 2)
        upper = slice(ROWS // 2, ROWS)
        fence = const.tile([P, 1], U32)

        with tc.manual_schedule():
            nc.scalar.activation(out=warm[:, 1:2], in_=warm[:, 0:1], func=SIN)
            pending = []
            for n in range(-2, UNITS):
                if n == -1:
                    turn_x(0)
                    quantise_x(0)
                    turn_x(1)
                    quantise_x(1)
                if 0 <= n + 1 < UNITS:
                    quantise(n + 1)
                    for b in range(BATCH):
                        multiply(n + 1, b)
                if n >= 0 and rotated(order[n]):
                    scaled = result.tile(
                        [P, 2, UNIT_HEADS, BATCH, PAIR, HEAD_DIM], F32, align_bytes=64, name="scaled"
                    )
                    if pending:
                        if n + 1 < UNITS:
                            nc.gpsimd.tensor_copy(out=fence[:], in_=packed_of[n + 1][0][:, 1024:1025])
                        sums(nc.gpsimd, pending[1], 0, every)
                        sums(nc.gpsimd, pending[1], 1, lower)
                    products(n, scaled)
                    if pending:
                        sums(nc.vector, pending[1], 1, upper)
                        for b in range(BATCH):
                            store(pending[0], pending[1], b)
                    pending = [n, scaled]
                elif n >= 0:
                    scaled = result.tile(
                        [P, 1, UNIT_HEADS, BATCH, PAIR, HEAD_DIM], F32, align_bytes=64, name="scaled"
                    )
                    for c in range(2):
                        for e in range(PAIR):
                            nc.scalar.copy(out=scaled[:, 0, :, c, e, :], in_=banks_of[(n, c, e)])
                        if n == UNITS - 1:
                            for b in range(BATCH):
                                store_half(n, scaled, b, c)
                    if n < UNITS - 1:
                        for b in range(BATCH):
                            store(n, scaled, b)
                if n == 2:
                    load_weights([8, 9, 10, 11])
                if n + 2 < UNITS:
                    regroup(n + 2, (1, 2) if n < 0 or not rotated(order[n]) else ())
                if n == -1:
                    make_factors()
                if n == ROPE_SECTIONS * UNITS_PER_SECTION - 1:
                    for s in range(2):
                        sums(nc.vector, pending[1], s, every)
                    for b in range(BATCH):
                        store(pending[0], pending[1], b)
